import numpy as np
import ml_dtypes


def mxq(x, axis, fmt="e4m3"):
    dtype, down = {"e4m3": (ml_dtypes.float8_e4m3fn, 7), "e5m2": (ml_dtypes.float8_e5m2, 14)}[fmt]
    v = np.moveaxis(np.asarray(x, np.float32).astype(ml_dtypes.bfloat16).astype(np.float64), axis, -1)
    blocks = v.reshape(v.shape[:-1] + (-1, 32))
    amax = np.abs(blocks).max(-1, keepdims=True)
    byte = np.maximum(np.where(amax > 0, np.frexp(amax)[1] - 1 + 127, 0) - down, 1)
    scale = np.exp2(byte - 127.0)
    codes = (blocks / scale).astype(np.float32).astype(dtype).astype(np.float64)
    return np.moveaxis((codes * scale).reshape(v.shape), -1, axis)


WIDE = False


def mx_kscale(k):
    if not WIDE:
        return np.ones(k)
    levels = np.array([10, -10, 5, -5, 0])
    a = np.random.permutation(np.resize(levels, k // 512 * 4)).reshape(k // 512, 4)
    idx = np.arange(k)
    return np.exp2(a[idx // 512, idx % 128 // 32])


BF16 = ml_dtypes.bfloat16


def bf(x):
    return np.asarray(x, np.float32).astype(BF16)


def f64(x):
    return np.asarray(x).astype(np.float64)


E2M1 = np.array([0.0, 0.5, 1.0, 1.5, 2.0, 3.0, 4.0, 6.0, -0.0, -0.5, -1.0, -1.5, -2.0, -3.0, -4.0, -6.0])


def pack_weight(w, fmt):
    k, n = w.shape
    w = f64(bf(w)).reshape(k // 32, 32, n)
    amax = np.abs(w).max(1)
    if fmt == "e4m3":
        byte = np.frexp(amax)[1] - 1 + 127 - 7
    else:
        mant, ex = np.frexp(amax / 6.0)
        byte = np.where(mant > 0.5, ex, ex - 1) + 127
    byte = np.clip(np.where(amax > 0, byte, 1), 1, 254)
    scaled = (w * np.exp2(127.0 - byte)[:, None, :]).reshape(k, n).astype(np.float32)
    by_word = np.ascontiguousarray(scaled.reshape(k // 512, 128, 4, n).transpose(0, 1, 3, 2))
    if fmt == "e4m3":
        words = by_word.astype(ml_dtypes.float8_e4m3fn).view(np.uint8)
    else:
        c = by_word.astype(ml_dtypes.float4_e2m1fn).view(np.uint8) & 0xF
        words = c[..., 0::2] | (c[..., 1::2] << 4)
    return np.ascontiguousarray(words), np.ascontiguousarray(byte.astype(np.uint8).reshape(k // 512, 16, n))


def unpack_weight(words, scales, fmt):
    g, p, n, _ = words.shape
    if fmt == "e4m3":
        vals = np.ascontiguousarray(words).view(ml_dtypes.float8_e4m3fn).astype(np.float64)
    else:
        nib = np.empty((g, p, n, 4), np.uint8)
        nib[..., 0::2] = words & 0xF
        nib[..., 1::2] = words >> 4
        vals = E2M1[nib]
    vals = vals * np.repeat(np.exp2(scales.astype(np.float64) - 127.0), 8, axis=1)[..., None]
    return vals.transpose(0, 1, 3, 2).reshape(g * 512, n)


B, T, E, Q = 4, 128, 256, 16384
N = B * T


def setup_inputs():
    s = mx_kscale(Q)
    y = bf(np.random.standard_normal((B, T, Q)) * s)
    w = np.random.standard_normal((2 * E, Q)) / np.sqrt(Q) / s
    words, scales = pack_weight(np.ascontiguousarray(w.T), "e4m3")
    return {"y": y, "w_swiglu_words": words, "w_swiglu_scales": scales}


def reference(y, w_swiglu_words, w_swiglu_scales):
    uv = mxq(f64(y).reshape(N, Q), 1, "e4m3") @ unpack_weight(w_swiglu_words, w_swiglu_scales, "e4m3")
    u, v = uv[:, :E], uv[:, E:]
    ao = mxq(u.T, 1, "e4m3") @ mxq(v, 0, "e4m3")
    return ao / B * E ** (-0.5)

@@ -1,0 +1,159 @@
+from contextlib import ExitStack
+
+import concourse.mybir as mybir
+from concourse.masks import make_identity
+
+F32 = mybir.dt.float32
+BF16 = mybir.dt.bfloat16
+I32 = mybir.dt.int32
+U32 = mybir.dt.uint32
+U8 = mybir.dt.uint8
+FP8X4 = mybir.dt.float8_e4m3fn_x4
+
+P = 128
+PACK = 4
+K_PASS = P * PACK
+
+BATCH, SEQ, E, Q = 4, 128, 256, 16384
+TOKENS = BATCH * SEQ
+TOKEN_TILES = TOKENS // P
+COLS = 2 * E
+PASSES = Q // K_PASS
+
+CHUNK = 4
+CHUNKS = PASSES // CHUNK
+PAIR = 2
+HALVES = TOKEN_TILES // PAIR
+ROUNDS = CHUNKS * HALVES
+PREFETCH = 6
+
+FLOPS = 2 * TOKENS * Q * COLS + 2 * E * E * TOKENS
+
+
+def tile_retentionmechanism_pa_k_kernel(tc, y, w_swiglu_words, w_swiglu_scales, out):
+    nc = tc.nc
+    y_rows = y.rearrange("b t q -> (b t) q").rearrange("(p j) q -> p j q", j=TOKEN_TILES)
+
+    with ExitStack() as ctx:
+        const = ctx.enter_context(tc.tile_pool(name="const", bufs=1))
+        w_pool = ctx.enter_context(tc.tile_pool(name="w", bufs=1))
+        raw_pool = ctx.enter_context(tc.tile_pool(name="raw", bufs=PREFETCH))
+        work = ctx.enter_context(tc.tile_pool(name="work", bufs=3))
+        last = ctx.enter_context(tc.tile_pool(name="last", bufs=1))
+        acc_pool = ctx.enter_context(tc.psum_pool(name="acc", bufs=1))
+        bank_pool = ctx.enter_context(tc.psum_pool(name="bank", bufs=4))
+        ctx.enter_context(tc.manual_schedule())
+
+        planes = const.tile([P, CHUNKS, COLS], U8, align_bytes=64)
+        nc.vector.memset(planes[:].rearrange("p c n -> p (c n)").bitcast(I32), 0)
+        ident = const.tile([P, P], F32)
+        make_identity(nc, ident[:])
+
+        uv_acc = [acc_pool.tile([P, COLS], F32, name="uv_acc%d" % j) for j in range(TOKEN_TILES)]
+        raw, w_words, y_codes, y_scales, grouped = {}, {}, {}, {}, {}
+
+        def load(r):
+            c, h = divmod(r, HALVES)
+            raw[r] = raw_pool.tile([P, PAIR, CHUNK * K_PASS], BF16, name="raw")
+            nc.sync.dma_start(
+                out=raw[r][:],
+                in_=y_rows[:, PAIR * h : PAIR * (h + 1), CHUNK * K_PASS * c : CHUNK * K_PASS * (c + 1)],
+            )
+            if h < HALVES - 1:
+                return
+            for s in range(4):
+                nc.sync.dma_start(
+                    out=planes[32 * s : 32 * s + 16, c, :].bitcast(I32),
+                    in_=w_swiglu_scales[CHUNK * c : CHUNK * (c + 1), 4 * s : 4 * s + 4, :].bitcast(I32),
+                )
+            w_words[c] = w_pool.tile([P, CHUNK, PACK * COLS], U8, name="w_words%d" % c, align_bytes=64)
+            nc.sync.dma_start(
+                out=w_words[c][:].bitcast(I32),
+                in_=w_swiglu_words[CHUNK * c : CHUNK * (c + 1)].rearrange("g p n t -> p g (n t)").bitcast(I32),
+            )
+
+        def transpose_round(r):
+            by_u = work.tile([P, PAIR * CHUNK, 2, P], F32, name="by_u")
+            nc.vector.tensor_copy(
+                out=by_u[:],
+                in_=raw[r][:].bitcast(F32).rearrange("p j (g m u) -> p (j g) u m", m=P, u=2),
+            )
+            if r + PREFETCH < ROUNDS:
+                load(r + PREFETCH)
+            grouped[r] = work.tile([P, CHUNK, PAIR, P, PACK], BF16, name="grouped", align_bytes=64)
+            for g in range(CHUNK):
+                bank = bank_pool.tile([P, PAIR, 2, P], F32, name="bank")
+                for j in range(PAIR):
+                    for u in range(2):
+                        nc.tensor.transpose(bank[:, j, u, :], by_u[:, CHUNK * j + g, u, :], ident[:])
+                nc.scalar.copy(
+                    out=grouped[r][:, g].bitcast(F32),
+                    in_=bank[:].rearrange("p j u m -> p j m u"),
+                )
+
+        def quantise_round(r):
+            y_codes[r] = work.tile([P, CHUNK * PAIR * P], U32, name="y_codes", align_bytes=64)
+            y_scales[r] = work.tile([P, CHUNK * PAIR * P], U8, name="y_scales", align_bytes=64)
+            width = CHUNK * PAIR * P // 2
+            for i in range(2):
+                nc.vector.quantize_mx(
+                    out=y_codes[r][:, width * i : width * (i + 1)].bitcast(FP8X4),
+                    scales=y_scales[r][:, width * i : width * (i + 1)],
+                    in_=grouped[r][:, 2 * i : 2 * i + 2].rearrange("p g j m t -> p (g j m t)"),
+                )
+
+        def multiply_round(r):
+            c, h = divmod(r, HALVES)
+            for g in range(CHUNK):
+                for j in range(PAIR):
+                    tokens = slice(P * (PAIR * g + j), P * (PAIR * g + j + 1))
+                    nc.tensor.matmul_mx(
+                        out=uv_acc[PAIR * h + j][:],
+                        lhsT=y_codes[r][:, tokens].bitcast(FP8X4),
+                        lhsT_scale=y_scales[r][:, tokens],
+                        rhs=w_words[c][:, g, :].bitcast(FP8X4),
+                        rhs_scale=planes[4 * g : P, c, :],
+                        start=(c == 0 and g == 0),
+                        stop=(c == CHUNKS - 1 and g == CHUNK - 1),
+                    )
+
+        for r in range(PREFETCH):
+            load(r)
+        transpose_round(0)
+        for r in range(ROUNDS):
+            if r + 1 < ROUNDS:
+                transpose_round(r + 1)
+            quantise_round(r)
+            multiply_round(r)
+
+        uv = last.tile([P, TOKEN_TILES, COLS], BF16)
+        for j in range(TOKEN_TILES):
+            if j % 2 == 0:
+                nc.scalar.copy(out=uv[:, j, :], in_=uv_acc[j][:])
+            else:
+                nc.vector.tensor_copy(out=uv[:, j, :], in_=uv_acc[j][:])
+        uv_grouped = last.tile([P, COLS, PACK], BF16, align_bytes=64)
+        nc.vector.tensor_copy(out=uv_grouped[:], in_=uv[:].rearrange("p j n -> p n j"))
+        uv_codes = last.tile([P, COLS], U32, align_bytes=64)
+        uv_scales = last.tile([P, COLS], U8, align_bytes=64)
+        nc.vector.quantize_mx(
+            out=uv_codes[:].bitcast(FP8X4),
+            scales=uv_scales[:],
+            in_=uv_grouped[:].rearrange("p n j -> p (n j)"),
+        )
+        factor = 1.0 / BATCH * E ** (-0.5)
+        for a in range(E // P):
+            d_cols = slice(P * a, P * (a + 1))
+            product = bank_pool.tile([P, E], F32, name="product", tag="bank")
+            nc.tensor.matmul_mx(
+                out=product[:],
+                lhsT=uv_codes[:, d_cols].bitcast(FP8X4),
+                lhsT_scale=uv_scales[:, d_cols],
+                rhs=uv_codes[:, E:COLS].bitcast(FP8X4),
+                rhs_scale=uv_scales[:, E:COLS],
+                start=True,
+                stop=True,
+            )
+            result = last.tile([P, E], F32, name="result%d" % a)
+            nc.vector.tensor_scalar_mul(out=result[:], in0=product[:], scalar1=factor)
+            nc.sync.dma_start(out=out[d_cols, :], in_=result[:])

@@ -37,7 +37,8 @@ def tile_retentionmechanism_pa_k_kernel(tc, y, w_swiglu_words, w_swiglu_scales, 
     with ExitStack() as ctx:
         const = ctx.enter_context(tc.tile_pool(name="const", bufs=1))
         w_pool = ctx.enter_context(tc.tile_pool(name="w", bufs=1))
-        raw_pool = ctx.enter_context(tc.tile_pool(name="raw", bufs=PREFETCH))
+        raw_pool = ctx.enter_context(tc.tile_pool(name="raw", bufs=PREFETCH * PAIR))
+        sort_pool = ctx.enter_context(tc.tile_pool(name="sort", bufs=2 * PAIR))
         work = ctx.enter_context(tc.tile_pool(name="work", bufs=3))
         last = ctx.enter_context(tc.tile_pool(name="last", bufs=1))
         acc_pool = ctx.enter_context(tc.psum_pool(name="acc", bufs=1))
@@ -52,15 +53,15 @@ def tile_retentionmechanism_pa_k_kernel(tc, y, w_swiglu_words, w_swiglu_scales, 
         uv_acc = [acc_pool.tile([P, COLS], F32, name="uv_acc%d" % j) for j in range(TOKEN_TILES)]
         raw, w_words, y_codes, y_scales, grouped = {}, {}, {}, {}, {}
 
-        def load(r):
+        def load_y(r, j):
             c, h = divmod(r, HALVES)
-            raw[r] = raw_pool.tile([P, PAIR, CHUNK * K_PASS], BF16, name="raw")
+            raw[r, j] = raw_pool.tile([P, CHUNK * K_PASS], BF16, name="raw")
             nc.sync.dma_start(
-                out=raw[r][:],
-                in_=y_rows[:, PAIR * h : PAIR * (h + 1), CHUNK * K_PASS * c : CHUNK * K_PASS * (c + 1)],
+                out=raw[r, j][:],
+                in_=y_rows[:, PAIR * h + j, CHUNK * K_PASS * c : CHUNK * K_PASS * (c + 1)],
             )
-            if h < HALVES - 1:
-                return
+
+        def load_w(c):
             for s in range(4):
                 nc.sync.dma_start(
                     out=planes[32 * s : 32 * s + 16, c, :].bitcast(I32),
@@ -72,45 +73,49 @@ def tile_retentionmechanism_pa_k_kernel(tc, y, w_swiglu_words, w_swiglu_scales, 
                 in_=w_swiglu_words[CHUNK * c : CHUNK * (c + 1)].rearrange("g p n t -> p g (n t)").bitcast(I32),
             )
 
+        def load(r, j):
+            load_y(r, j)
+            if r % HALVES == HALVES - 1 and j == PAIR - 1:
+                load_w(r // HALVES)
+
         def transpose_round(r):
-            by_u = work.tile([P, PAIR * CHUNK, 2, P], F32, name="by_u")
-            nc.vector.tensor_copy(
-                out=by_u[:],
-                in_=raw[r][:].bitcast(F32).rearrange("p j (g m u) -> p (j g) u m", m=P, u=2),
-            )
-            if r + PREFETCH < ROUNDS:
-                load(r + PREFETCH)
-            grouped[r] = work.tile([P, CHUNK, PAIR, P, PACK], BF16, name="grouped", align_bytes=64)
-            for g in range(CHUNK):
-                bank = bank_pool.tile([P, PAIR, 2, P], F32, name="bank")
-                for j in range(PAIR):
-                    for u in range(2):
-                        nc.tensor.transpose(bank[:, j, u, :], by_u[:, CHUNK * j + g, u, :], ident[:])
-                nc.scalar.copy(
-                    out=grouped[r][:, g].bitcast(F32),
-                    in_=bank[:].rearrange("p j u m -> p j m u"),
+            grouped[r] = work.tile([P, PAIR, CHUNK, P, PACK], BF16, name="grouped", align_bytes=64)
+            for j in range(PAIR):
+                by_u = sort_pool.tile([P, CHUNK, 2, P], F32, name="by_u")
+                nc.vector.tensor_copy(
+                    out=by_u[:],
+                    in_=raw[r, j][:].bitcast(F32).rearrange("p (g m u) -> p g u m", m=P, u=2),
                 )
+                if r + PREFETCH < ROUNDS:
+                    load(r + PREFETCH, j)
+                for g in range(0, CHUNK, 2):
+                    bank = bank_pool.tile([P, 2, 2, P], F32, name="bank")
+                    for i in range(2):
+                        for u in range(2):
+                            nc.tensor.transpose(bank[:, i, u, :], by_u[:, g + i, u, :], ident[:])
+                    nc.scalar.copy(
+                        out=grouped[r][:, j, g : g + 2].bitcast(F32),
+                        in_=bank[:].rearrange("p i u m -> p i m u"),
+                    )
 
         def quantise_round(r):
-            y_codes[r] = work.tile([P, CHUNK * PAIR * P], U32, name="y_codes", align_bytes=64)
-            y_scales[r] = work.tile([P, CHUNK * PAIR * P], U8, name="y_scales", align_bytes=64)
-            width = CHUNK * PAIR * P // 2
-            for i in range(2):
+            y_codes[r] = work.tile([P, PAIR, CHUNK * P], U32, name="y_codes", align_bytes=64)
+            y_scales[r] = work.tile([P, PAIR, CHUNK * P], U8, name="y_scales", align_bytes=64)
+            for j in range(PAIR):
                 nc.vector.quantize_mx(
-                    out=y_codes[r][:, width * i : width * (i + 1)].bitcast(FP8X4),
-                    scales=y_scales[r][:, width * i : width * (i + 1)],
-                    in_=grouped[r][:, 2 * i : 2 * i + 2].rearrange("p g j m t -> p (g j m t)"),
+                    out=y_codes[r][:, j, :].bitcast(FP8X4),
+                    scales=y_scales[r][:, j, :],
+                    in_=grouped[r][:, j].rearrange("p g m t -> p (g m t)"),
                 )
 
         def multiply_round(r):
             c, h = divmod(r, HALVES)
-            for g in range(CHUNK):
-                for j in range(PAIR):
-                    tokens = slice(P * (PAIR * g + j), P * (PAIR * g + j + 1))
+            for j in range(PAIR):
+                for g in range(CHUNK):
                     nc.tensor.matmul_mx(
                         out=uv_acc[PAIR * h + j][:],
-                        lhsT=y_codes[r][:, tokens].bitcast(FP8X4),
-                        lhsT_scale=y_scales[r][:, tokens],
+                        lhsT=y_codes[r][:, j, P * g : P * (g + 1)].bitcast(FP8X4),
+                        lhsT_scale=y_scales[r][:, j, P * g : P * (g + 1)],
                         rhs=w_words[c][:, g, :].bitcast(FP8X4),
                         rhs_scale=planes[4 * g : P, c, :],
                         start=(c == 0 and g == 0),
@@ -118,7 +123,8 @@ def tile_retentionmechanism_pa_k_kernel(tc, y, w_swiglu_words, w_swiglu_scales, 
                     )
 
         for r in range(PREFETCH):
-            load(r)
+            for j in range(PAIR):
+                load(r, j)
         transpose_round(0)
         for r in range(ROUNDS):
             if r + 1 < ROUNDS:
@@ -133,7 +139,10 @@ def tile_retentionmechanism_pa_k_kernel(tc, y, w_swiglu_words, w_swiglu_scales, 
             else:
                 nc.vector.tensor_copy(out=uv[:, j, :], in_=uv_acc[j][:])
         uv_grouped = last.tile([P, COLS, PACK], BF16, align_bytes=64)
-        nc.vector.tensor_copy(out=uv_grouped[:], in_=uv[:].rearrange("p j n -> p n j"))
+        nc.vector.tensor_copy(
+            out=uv_grouped[:].rearrange("p (n i) j -> p n j i", i=4),
+            in_=uv[:].rearrange("p j (n i) -> p n j i", i=4),
+        )
         uv_codes = last.tile([P, COLS], U32, align_bytes=64)
         uv_scales = last.tile([P, COLS], U8, align_bytes=64)
         nc.vector.quantize_mx(

@@ -46,12 +46,17 @@ def tile_retentionmechanism_pa_k_kernel(tc, y, w_swiglu_words, w_swiglu_scales, 
         ctx.enter_context(tc.manual_schedule())
 
         planes = const.tile([P, CHUNKS, COLS], U8, align_bytes=64)
+        zeros = const.tile([P, COLS], BF16)
+        nc.vector.memset(zeros[:], 0.0)
         nc.vector.memset(planes[:].rearrange("p c n -> p (c n)").bitcast(I32), 0)
         ident = const.tile([P, P], F32)
         make_identity(nc, ident[:])
 
         uv_acc = [acc_pool.tile([P, COLS], F32, name="uv_acc%d" % j) for j in range(TOKEN_TILES)]
         raw, w_words, y_codes, y_scales, grouped = {}, {}, {}, {}, {}
+
+        def keep_busy(bank):
+            nc.tensor.matmul(bank[:], lhsT=zeros[:, :P], rhs=zeros[:], start=True, stop=True)
 
         def load_y(r, j):
             c, h = divmod(r, HALVES)
@@ -68,10 +73,12 @@ def tile_retentionmechanism_pa_k_kernel(tc, y, w_swiglu_words, w_swiglu_scales, 
                     in_=w_swiglu_scales[CHUNK * c : CHUNK * (c + 1), 4 * s : 4 * s + 4, :].bitcast(I32),
                 )
             w_words[c] = w_pool.tile([P, CHUNK, PACK * COLS], U8, name="w_words%d" % c, align_bytes=64)
-            nc.sync.dma_start(
-                out=w_words[c][:].bitcast(I32),
-                in_=w_swiglu_words[CHUNK * c : CHUNK * (c + 1)].rearrange("g p n t -> p g (n t)").bitcast(I32),
-            )
+            for g in range(0, CHUNK, 2):
+                words = w_swiglu_words[CHUNK * c + g : CHUNK * c + g + 2]
+                nc.sync.dma_start(
+                    out=w_words[c][:, g : g + 2, :].bitcast(I32),
+                    in_=words.rearrange("g p n t -> p g (n t)").bitcast(I32),
+                )
 
         def load(r, j):
             load_y(r, j)
@@ -125,6 +132,8 @@ def tile_retentionmechanism_pa_k_kernel(tc, y, w_swiglu_words, w_swiglu_scales, 
         for r in range(PREFETCH):
             for j in range(PAIR):
                 load(r, j)
+        for i in range(7):
+            keep_busy(uv_acc[-1])
         transpose_round(0)
         for r in range(ROUNDS):
             if r + 1 < ROUNDS:
@@ -132,24 +141,35 @@ def tile_retentionmechanism_pa_k_kernel(tc, y, w_swiglu_words, w_swiglu_scales, 
             quantise_round(r)
             multiply_round(r)
 
+        idle = bank_pool.tile([P, COLS], F32, name="idle", tag="bank")
+        for i in range(7):
+            keep_busy(idle)
+
         uv = last.tile([P, TOKEN_TILES, COLS], BF16)
-        for j in range(TOKEN_TILES):
-            if j % 2 == 0:
-                nc.scalar.copy(out=uv[:, j, :], in_=uv_acc[j][:])
-            else:
-                nc.vector.tensor_copy(out=uv[:, j, :], in_=uv_acc[j][:])
+        nc.scalar.copy(out=uv[:, 0, :], in_=uv_acc[0][:])
+        nc.vector.tensor_copy(out=uv[:, 1, :], in_=uv_acc[1][:])
+        nc.scalar.copy(out=uv[:, 2, :], in_=uv_acc[2][:])
+        nc.vector.tensor_copy(out=uv[:, 3, E:COLS], in_=uv_acc[3][:, E:COLS])
+        nc.scalar.copy(out=uv[:, 3, 0:E], in_=uv_acc[3][:, 0:E])
         uv_grouped = last.tile([P, COLS, PACK], BF16, align_bytes=64)
-        nc.vector.tensor_copy(
-            out=uv_grouped[:].rearrange("p (n i) j -> p n j i", i=4),
-            in_=uv[:].rearrange("p j (n i) -> p n j i", i=4),
-        )
+
+        def regroup(copy, cols):
+            copy(
+                out=uv_grouped[:, cols, :].rearrange("p (n i) j -> p n j i", i=4),
+                in_=uv[:, :, cols].rearrange("p j (n i) -> p n j i", i=4),
+            )
+
+        regroup(nc.vector.tensor_copy, slice(E, COLS))
+        regroup(nc.scalar.copy, slice(0, P))
+        regroup(nc.vector.tensor_copy, slice(P, E))
         uv_codes = last.tile([P, COLS], U32, align_bytes=64)
         uv_scales = last.tile([P, COLS], U8, align_bytes=64)
-        nc.vector.quantize_mx(
-            out=uv_codes[:].bitcast(FP8X4),
-            scales=uv_scales[:],
-            in_=uv_grouped[:].rearrange("p n j -> p (n j)"),
-        )
+        for cols in (slice(E, COLS), slice(0, E)):
+            nc.vector.quantize_mx(
+                out=uv_codes[:, cols].bitcast(FP8X4),
+                scales=uv_scales[:, cols],
+                in_=uv_grouped[:, cols, :].rearrange("p n j -> p (n j)"),
+            )
         factor = 1.0 / BATCH * E ** (-0.5)
         for a in range(E // P):
             d_cols = slice(P * a, P * (a + 1))
@@ -164,5 +184,9 @@ def tile_retentionmechanism_pa_k_kernel(tc, y, w_swiglu_words, w_swiglu_scales, 
                 stop=True,
             )
             result = last.tile([P, E], F32, name="result%d" % a)
-            nc.vector.tensor_scalar_mul(out=result[:], in0=product[:], scalar1=factor)
-            nc.sync.dma_start(out=out[d_cols, :], in_=result[:])
+            if a == 0:
+                nc.scalar.mul(result[:], product[:], factor)
+                nc.scalar.dma_start(out=out[d_cols, :], in_=result[:])
+            else:
+                nc.vector.tensor_scalar_mul(out=result[:], in0=product[:], scalar1=factor)
+                nc.sync.dma_start(out=out[d_cols, :], in_=result[:])

@@ -132,8 +132,6 @@ def tile_retentionmechanism_pa_k_kernel(tc, y, w_swiglu_words, w_swiglu_scales, 
         for r in range(PREFETCH):
             for j in range(PAIR):
                 load(r, j)
-        for i in range(7):
-            keep_busy(uv_acc[-1])
         transpose_round(0)
         for r in range(ROUNDS):
             if r + 1 < ROUNDS:
@@ -142,29 +140,25 @@ def tile_retentionmechanism_pa_k_kernel(tc, y, w_swiglu_words, w_swiglu_scales, 
             multiply_round(r)
 
         idle = bank_pool.tile([P, COLS], F32, name="idle", tag="bank")
-        for i in range(7):
+        for i in range(5):
             keep_busy(idle)
 
         uv = last.tile([P, TOKEN_TILES, COLS], BF16)
+        u_cols, v_cols = slice(0, E), slice(E, COLS)
         nc.scalar.copy(out=uv[:, 0, :], in_=uv_acc[0][:])
         nc.vector.tensor_copy(out=uv[:, 1, :], in_=uv_acc[1][:])
         nc.scalar.copy(out=uv[:, 2, :], in_=uv_acc[2][:])
-        nc.vector.tensor_copy(out=uv[:, 3, E:COLS], in_=uv_acc[3][:, E:COLS])
-        nc.scalar.copy(out=uv[:, 3, 0:E], in_=uv_acc[3][:, 0:E])
+        nc.vector.tensor_copy(out=uv[:, 3, v_cols], in_=uv_acc[3][:, v_cols])
+        nc.scalar.copy(out=uv[:, 3, u_cols], in_=uv_acc[3][:, u_cols])
         uv_grouped = last.tile([P, COLS, PACK], BF16, align_bytes=64)
-
-        def regroup(copy, cols):
-            copy(
+        for cols in (v_cols, u_cols):
+            nc.vector.tensor_copy(
                 out=uv_grouped[:, cols, :].rearrange("p (n i) j -> p n j i", i=4),
                 in_=uv[:, :, cols].rearrange("p j (n i) -> p n j i", i=4),
             )
-
-        regroup(nc.vector.tensor_copy, slice(E, COLS))
-        regroup(nc.scalar.copy, slice(0, P))
-        regroup(nc.vector.tensor_copy, slice(P, E))
         uv_codes = last.tile([P, COLS], U32, align_bytes=64)
         uv_scales = last.tile([P, COLS], U8, align_bytes=64)
-        for cols in (slice(E, COLS), slice(0, E)):
+        for cols in (v_cols, u_cols):
             nc.vector.quantize_mx(
                 out=uv_codes[:, cols].bitcast(FP8X4),
                 scales=uv_scales[:, cols],
@@ -184,9 +178,5 @@ def tile_retentionmechanism_pa_k_kernel(tc, y, w_swiglu_words, w_swiglu_scales, 
                 stop=True,
             )
             result = last.tile([P, E], F32, name="result%d" % a)
-            if a == 0:
-                nc.scalar.mul(result[:], product[:], factor)
-                nc.scalar.dma_start(out=out[d_cols, :], in_=result[:])
-            else:
-                nc.vector.tensor_scalar_mul(out=result[:], in0=product[:], scalar1=factor)
-                nc.sync.dma_start(out=out[d_cols, :], in_=result[:])
+            nc.vector.tensor_scalar_mul(out=result[:], in0=product[:], scalar1=factor)
+            nc.sync.dma_start(out=out[d_cols, :], in_=result[:])

from contextlib import ExitStack

import concourse.mybir as mybir
from concourse.masks import make_identity

F32 = mybir.dt.float32
BF16 = mybir.dt.bfloat16
I32 = mybir.dt.int32
U32 = mybir.dt.uint32
U8 = mybir.dt.uint8
FP8X4 = mybir.dt.float8_e4m3fn_x4

P = 128
PACK = 4
K_PASS = P * PACK

BATCH, SEQ, E, Q = 4, 128, 256, 16384
TOKENS = BATCH * SEQ
TOKEN_TILES = TOKENS // P
COLS = 2 * E
PASSES = Q // K_PASS

CHUNK = 4
CHUNKS = PASSES // CHUNK
PAIR = 2
HALVES = TOKEN_TILES // PAIR
ROUNDS = CHUNKS * HALVES
PREFETCH = 6

FLOPS = 2 * TOKENS * Q * COLS + 2 * E * E * TOKENS


def tile_retentionmechanism_pa_k_kernel(tc, y, w_swiglu_words, w_swiglu_scales, out):
    nc = tc.nc
    y_rows = y.rearrange("b t q -> (b t) q").rearrange("(p j) q -> p j q", j=TOKEN_TILES)

    with ExitStack() as ctx:
        const = ctx.enter_context(tc.tile_pool(name="const", bufs=1))
        w_pool = ctx.enter_context(tc.tile_pool(name="w", bufs=1))
        raw_pool = ctx.enter_context(tc.tile_pool(name="raw", bufs=PREFETCH * PAIR))
        sort_pool = ctx.enter_context(tc.tile_pool(name="sort", bufs=2 * PAIR))
        work = ctx.enter_context(tc.tile_pool(name="work", bufs=3))
        last = ctx.enter_context(tc.tile_pool(name="last", bufs=1))
        acc_pool = ctx.enter_context(tc.psum_pool(name="acc", bufs=1))
        bank_pool = ctx.enter_context(tc.psum_pool(name="bank", bufs=4))
        ctx.enter_context(tc.manual_schedule())

        planes = const.tile([P, CHUNKS, COLS], U8, align_bytes=64)
        zeros = const.tile([P, COLS], BF16)
        nc.vector.memset(zeros[:], 0.0)
        nc.vector.memset(planes[:].rearrange("p c n -> p (c n)").bitcast(I32), 0)
        ident = const.tile([P, P], F32)
        make_identity(nc, ident[:])

        uv_acc = [acc_pool.tile([P, COLS], F32, name="uv_acc%d" % j) for j in range(TOKEN_TILES)]
        raw, w_words, y_codes, y_scales, grouped = {}, {}, {}, {}, {}

        def keep_busy(bank):
            nc.tensor.matmul(bank[:], lhsT=zeros[:, :P], rhs=zeros[:], start=True, stop=True)

        def load_y(r, j):
            c, h = divmod(r, HALVES)
            raw[r, j] = raw_pool.tile([P, CHUNK * K_PASS], BF16, name="raw")
            nc.sync.dma_start(
                out=raw[r, j][:],
                in_=y_rows[:, PAIR * h + j, CHUNK * K_PASS * c : CHUNK * K_PASS * (c + 1)],
            )

        def load_w(c):
            for s in range(4):
                nc.sync.dma_start(
                    out=planes[32 * s : 32 * s + 16, c, :].bitcast(I32),
                    in_=w_swiglu_scales[CHUNK * c : CHUNK * (c + 1), 4 * s : 4 * s + 4, :].bitcast(I32),
                )
            w_words[c] = w_pool.tile([P, CHUNK, PACK * COLS], U8, name="w_words%d" % c, align_bytes=64)
            for g in range(0, CHUNK, 2):
                words = w_swiglu_words[CHUNK * c + g : CHUNK * c + g + 2]
                nc.sync.dma_start(
                    out=w_words[c][:, g : g + 2, :].bitcast(I32),
                    in_=words.rearrange("g p n t -> p g (n t)").bitcast(I32),
                )

        def load(r, j):
            load_y(r, j)
            if r % HALVES == HALVES - 1 and j == PAIR - 1:
                load_w(r // HALVES)

        def transpose_round(r):
            grouped[r] = work.tile([P, PAIR, CHUNK, P, PACK], BF16, name="grouped", align_bytes=64)
            for j in range(PAIR):
                by_u = sort_pool.tile([P, CHUNK, 2, P], F32, name="by_u")
                nc.vector.tensor_copy(
                    out=by_u[:],
                    in_=raw[r, j][:].bitcast(F32).rearrange("p (g m u) -> p g u m", m=P, u=2),
                )
                if r + PREFETCH < ROUNDS:
                    load(r + PREFETCH, j)
                for g in range(0, CHUNK, 2):
                    bank = bank_pool.tile([P, 2, 2, P], F32, name="bank")
                    for i in range(2):
                        for u in range(2):
                            nc.tensor.transpose(bank[:, i, u, :], by_u[:, g + i, u, :], ident[:])
                    nc.scalar.copy(
                        out=grouped[r][:, j, g : g + 2].bitcast(F32),
                        in_=bank[:].rearrange("p i u m -> p i m u"),
                    )

        def quantise_round(r):
            y_codes[r] = work.tile([P, PAIR, CHUNK * P], U32, name="y_codes", align_bytes=64)
            y_scales[r] = work.tile([P, PAIR, CHUNK * P], U8, name="y_scales", align_bytes=64)
            for j in range(PAIR):
                nc.vector.quantize_mx(
                    out=y_codes[r][:, j, :].bitcast(FP8X4),
                    scales=y_scales[r][:, j, :],
                    in_=grouped[r][:, j].rearrange("p g m t -> p (g m t)"),
                )

        def multiply_round(r):
            c, h = divmod(r, HALVES)
            for j in range(PAIR):
                for g in range(CHUNK):
                    nc.tensor.matmul_mx(
                        out=uv_acc[PAIR * h + j][:],
                        lhsT=y_codes[r][:, j, P * g : P * (g + 1)].bitcast(FP8X4),
                        lhsT_scale=y_scales[r][:, j, P * g : P * (g + 1)],
                        rhs=w_words[c][:, g, :].bitcast(FP8X4),
                        rhs_scale=planes[4 * g : P, c, :],
                        start=(c == 0 and g == 0),
                        stop=(c == CHUNKS - 1 and g == CHUNK - 1),
                    )

        for r in range(PREFETCH):
            for j in range(PAIR):
                load(r, j)
        transpose_round(0)
        for r in range(ROUNDS):
            if r + 1 < ROUNDS:
                transpose_round(r + 1)
            quantise_round(r)
            multiply_round(r)

        idle = bank_pool.tile([P, COLS], F32, name="idle", tag="bank")
        for i in range(5):
            keep_busy(idle)

        uv = last.tile([P, TOKEN_TILES, COLS], BF16)
        u_cols, v_cols = slice(0, E), slice(E, COLS)
        nc.scalar.copy(out=uv[:, 0, :], in_=uv_acc[0][:])
        nc.vector.tensor_copy(out=uv[:, 1, :], in_=uv_acc[1][:])
        nc.scalar.copy(out=uv[:, 2, :], in_=uv_acc[2][:])
        nc.vector.tensor_copy(out=uv[:, 3, v_cols], in_=uv_acc[3][:, v_cols])
        nc.scalar.copy(out=uv[:, 3, u_cols], in_=uv_acc[3][:, u_cols])
        uv_grouped = last.tile([P, COLS, PACK], BF16, align_bytes=64)
        for cols in (v_cols, u_cols):
            nc.vector.tensor_copy(
                out=uv_grouped[:, cols, :].rearrange("p (n i) j -> p n j i", i=4),
                in_=uv[:, :, cols].rearrange("p j (n i) -> p n j i", i=4),
            )
        uv_codes = last.tile([P, COLS], U32, align_bytes=64)
        uv_scales = last.tile([P, COLS], U8, align_bytes=64)
        for cols in (v_cols, u_cols):
            nc.vector.quantize_mx(
                out=uv_codes[:, cols].bitcast(FP8X4),
                scales=uv_scales[:, cols],
                in_=uv_grouped[:, cols, :].rearrange("p n j -> p (n j)"),
            )
        factor = 1.0 / BATCH * E ** (-0.5)
        for a in range(E // P):
            d_cols = slice(P * a, P * (a + 1))
            product = bank_pool.tile([P, E], F32, name="product", tag="bank")
            nc.tensor.matmul_mx(
                out=product[:],
                lhsT=uv_codes[:, d_cols].bitcast(FP8X4),
                lhsT_scale=uv_scales[:, d_cols],
                rhs=uv_codes[:, E:COLS].bitcast(FP8X4),
                rhs_scale=uv_scales[:, E:COLS],
                start=True,
                stop=True,
            )
            result = last.tile([P, E], F32, name="result%d" % a)
            nc.vector.tensor_scalar_mul(out=result[:], in0=product[:], scalar1=factor)
            nc.sync.dma_start(out=out[d_cols, :], in_=result[:])
